import numpy as np
import ml_dtypes


def mxq(x, axis, fmt="e4m3"):
    dtype, down = {"e4m3": (ml_dtypes.float8_e4m3fn, 7), "e5m2": (ml_dtypes.float8_e5m2, 14)}[fmt]
    v = np.moveaxis(np.asarray(x, np.float32).astype(ml_dtypes.bfloat16).astype(np.float64), axis, -1)
    blocks = v.reshape(v.shape[:-1] + (-1, 32))
    amax = np.abs(blocks).max(-1, keepdims=True)
    byte = np.maximum(np.where(amax > 0, np.frexp(amax)[1] - 1 + 127, 0) - down, 1)
    scale = np.exp2(byte - 127.0)
    codes = (blocks / scale).astype(np.float32).astype(dtype).astype(np.float64)
    return np.moveaxis((codes * scale).reshape(v.shape), -1, axis)


WIDE = False


def mx_kscale(k):
    if not WIDE:
        return np.ones(k)
    levels = np.array([10, -10, 5, -5, 0])
    a = np.random.permutation(np.resize(levels, k // 512 * 4)).reshape(k // 512, 4)
    idx = np.arange(k)
    return np.exp2(a[idx // 512, idx % 128 // 32])


BF16 = ml_dtypes.bfloat16


def bf(x):
    return np.asarray(x, np.float32).astype(BF16)


def f64(x):
    return np.asarray(x).astype(np.float64)


B, T, D, H, QB = 8, 512, 512, 4, 512
DH = D // H
HP = H // 2
EPS = 1e-6
LAYER_DEPTH = 6
LAMBDA_INIT = 0.8 - 0.6 * np.exp(-0.3 * LAYER_DEPTH)


def silu(u):
    return u / (1.0 + np.exp(-u))


def rmsnorm(u):
    return u / np.sqrt(np.mean(u * u, axis=-1, keepdims=True) + EPS)


def causal_attn(q, k, vq):
    rows = []
    for i in range(T // QB):
        n = (i + 1) * QB
        s = q[:, :, i * QB:n] @ k[:, :, :n].transpose(0, 1, 3, 2) * DH ** -0.5
        keep = np.arange(n)[None, :] <= np.arange(i * QB, n)[:, None]
        s = np.where(keep, s, -np.inf)
        e = np.exp(s - s.max(-1, keepdims=True))
        rows.append((mxq(e, 3, "e4m3") @ vq[:, :, :n]) / e.sum(-1, keepdims=True))
    return np.concatenate(rows, axis=2)


def setup_inputs():
    s = mx_kscale(D)
    qn = np.random.standard_normal((B, T, H, DH))
    kn = np.random.standard_normal((B, T, H, DH))
    return {"q_rot": bf(qn / np.sqrt(np.mean(qn * qn, axis=-1, keepdims=True))),
            "k_rot": bf(kn / np.sqrt(np.mean(kn * kn, axis=-1, keepdims=True))),
            "v": bf(np.random.standard_normal((B, T, HP, 2 * DH))),
            "hidden_states": bf(np.random.standard_normal((B, T, D)) * s),
            "W_g": bf(np.random.standard_normal((D, D)) / np.sqrt(D) / s[:, None]),
            "lambda_q1": bf(np.random.standard_normal((HP, DH // 2)) * 0.2),
            "lambda_k1": bf(np.random.standard_normal((HP, DH // 2)) * 0.2),
            "lambda_q2": bf(np.random.standard_normal((HP, DH // 2)) * 0.2),
            "lambda_k2": bf(np.random.standard_normal((HP, DH // 2)) * 0.2)}


def reference(q_rot, k_rot, v, hidden_states, W_g, lambda_q1, lambda_k1, lambda_q2, lambda_k2):
    q = f64(q_rot).transpose(0, 2, 1, 3)
    k = f64(k_rot).transpose(0, 2, 1, 3)
    vq = mxq(f64(v).transpose(0, 2, 1, 3), 2, "e4m3")
    y1 = causal_attn(q[:, 0::2], k[:, 0::2], vq)
    y2 = causal_attn(q[:, 1::2], k[:, 1::2], vq)
    lam1 = np.exp(np.sum(f64(lambda_q1) * f64(lambda_k1), axis=-1))
    lam2 = np.exp(np.sum(f64(lambda_q2) * f64(lambda_k2), axis=-1))
    lam = (lam1 - lam2 + LAMBDA_INIT)[None, :, None, None]
    y = (y1 - lam * y2).transpose(0, 2, 1, 3)
    x = f64(hidden_states).reshape(B * T, D)
    g = silu(mxq(x, 1, "e4m3") @ mxq(f64(W_g), 0, "e4m3")).reshape(B, T, HP, 2 * DH)
    y = rmsnorm(y * g) * (1.0 - LAMBDA_INIT)
    return y.reshape(B, T, D)

@@ -1,0 +1,395 @@
+import math
+from contextlib import ExitStack
+
+import concourse.mybir as mybir
+from concourse.masks import make_identity
+
+F32 = mybir.dt.float32
+BF16 = mybir.dt.bfloat16
+U32 = mybir.dt.uint32
+U8 = mybir.dt.uint8
+FP8X4 = mybir.dt.float8_e4m3fn_x4
+ACT = mybir.ActivationFunctionType
+ALU = mybir.AluOpType
+AX = mybir.AxisListType
+
+B, T, D, H = 8, 512, 512, 4
+DH = D // H
+HP = H // 2
+DV = 2 * DH
+P = 128
+PACK = 4
+QT = T // P
+LAM_LEN = DH // 2
+
+EPS = 1e-6
+LAMBDA_INIT = 0.8 - 0.6 * math.exp(-0.3 * 6)
+SCALE = DH ** -0.5
+MASKED = -1e30
+
+N_GROUPS = B * QT
+assert H == QT
+
+FLOPS = 2 * B * H * T * T * DH + 2 * B * H * T * T * DV + 2 * B * T * D * D
+
+
+def interleave_rows(nc, grouped, rows):
+    nc.vector.tensor_copy(
+        out=grouped.rearrange("p (c i) t -> p c t i", i=4),
+        in_=rows.rearrange("p t (c i) -> p c t i", i=4),
+    )
+
+
+def in_range(g):
+    return 0 <= g < N_GROUPS
+
+
+def query_tile(g, pair):
+    j = g % QT
+    return j if pair == 0 else QT - 1 - j
+
+
+def tile_mixerdiffattention_pb_t_kernel(
+    tc, q_rot, k_rot, v, hidden_states, W_g, lambda_q1, lambda_k1, lambda_q2, lambda_k2, out
+):
+    nc = tc.nc
+    with ExitStack() as ctx:
+        consts = ctx.enter_context(tc.tile_pool(name="consts", bufs=1))
+        loads = ctx.enter_context(tc.tile_pool(name="loads", bufs=2))
+        batch = ctx.enter_context(tc.tile_pool(name="batch", bufs=2))
+        work = ctx.enter_context(tc.tile_pool(name="work", bufs=3))
+        tail = ctx.enter_context(tc.tile_pool(name="tail", bufs=3))
+        small = ctx.enter_context(tc.tile_pool(name="small", bufs=6))
+        ps_s = ctx.enter_context(tc.psum_pool(name="ps_s", bufs=4))
+        ps_t = ctx.enter_context(tc.psum_pool(name="ps_t", bufs=2))
+        ps_y = ctx.enter_context(tc.psum_pool(name="ps_y", bufs=2))
+
+        def load_x(b):
+            x_sb = loads.tile([P, QT, D], BF16, name="x_sb", bufs=3)
+            nc.sync.dma_start(out=x_sb[:], in_=hidden_states[b].rearrange("(i p) k -> p i k", p=P))
+            return x_sb
+
+        def load_qkv(b):
+            q_sb = loads.tile([P, QT, D], BF16, name="q_sb")
+            k_sb = loads.tile([P, QT, D], BF16, name="k_sb")
+            v_sb = loads.tile([P, PACK, D], BF16, name="v_sb")
+            nc.sync.dma_start(out=q_sb[:], in_=q_rot[b].rearrange("(i p) h d -> p i (h d)", p=P))
+            nc.sync.dma_start(out=k_sb[:], in_=k_rot[b].rearrange("(i p) h d -> p i (h d)", p=P))
+            nc.sync.dma_start(out=v_sb[:], in_=v[b].rearrange("(t p) h c -> p t (h c)", p=P))
+            return q_sb, k_sb, v_sb
+
+        w_sb = consts.tile([P, PACK, D], BF16)
+        nc.sync.dma_start(
+            out=w_sb[:].rearrange("p (u e) n -> p u (e n)", u=2),
+            in_=W_g.rearrange("(u p e) n -> p u (e n)", u=2, e=2),
+        )
+        x_of = {0: load_x(0)}
+        lam_in = consts.tile([P, 2, 2, HP * LAM_LEN], BF16)
+        for j, vec in enumerate((lambda_q1, lambda_k1, lambda_q2, lambda_k2)):
+            nc.sync.dma_start(
+                out=lam_in[:, j // 2, j % 2, :],
+                in_=vec.rearrange("h j -> (h j)").partition_broadcast(P),
+            )
+        x_of[1] = load_x(1)
+        x_of[2] = load_x(2)
+        qkv_of = {0: load_qkv(0)}
+
+        ident_f32 = consts.tile([P, P], F32)
+        make_identity(nc, ident_f32[:])
+        ident_bf = consts.tile([P, P], BF16)
+        make_identity(nc, ident_bf[:])
+        mask_f32 = consts.tile([P, P], F32)
+        nc.gpsimd.memset(mask_f32[:], 0.0)
+        nc.gpsimd.affine_select(
+            out=mask_f32[:], in_=mask_f32[:], pattern=[[-1, P]], compare_op=ALU.is_ge,
+            fill=MASKED, base=0, channel_multiplier=1,
+        )
+        minus_half = consts.tile([P, HP], F32)
+        nc.vector.memset(minus_half[:], -0.5)
+        e_grp = [consts.tile([P, H, P, PACK], BF16, name="e_grp%d" % j, align_bytes=64) for j in range(QT)]
+        for j in range(QT):
+            nc.gpsimd.memset(e_grp[j][:], 0.0)
+
+        w_grp = consts.tile([P, D, PACK], BF16, align_bytes=64)
+        interleave_rows(nc, w_grp[:], w_sb[:])
+        mask_bf = consts.tile([P, P], BF16)
+        nc.vector.tensor_copy(out=mask_bf[:], in_=mask_f32[:])
+        w_codes = consts.tile([P, D], U32, align_bytes=64)
+        w_scales = consts.tile([P, D], U8, align_bytes=64)
+        nc.vector.quantize_mx(
+            out=w_codes[:].bitcast(FP8X4), scales=w_scales[:], in_=w_grp[:].rearrange("p n t -> p (n t)")
+        )
+
+        lam_prod = consts.tile([P, 2, HP * LAM_LEN], F32)
+        nc.vector.tensor_tensor(out=lam_prod[:], in0=lam_in[:, :, 0, :], in1=lam_in[:, :, 1, :], op=ALU.mult)
+        lam_dot = consts.tile([P, 2 * HP], F32)
+        nc.vector.tensor_reduce(
+            out=lam_dot[:], in_=lam_prod[:].rearrange("p s (h j) -> p (s h) j", h=HP), axis=AX.X, op=ALU.add
+        )
+        lam_exp = consts.tile([P, 2 * HP], F32)
+        nc.scalar.activation(out=lam_exp[:], in_=lam_dot[:], func=ACT.Exp)
+        neg_lam = consts.tile([P, HP], F32)
+        nc.vector.scalar_tensor_tensor(
+            out=neg_lam[:], in0=lam_exp[:, HP : 2 * HP], scalar=-LAMBDA_INIT, in1=lam_exp[:, 0:HP],
+            op0=ALU.add, op1=ALU.subtract,
+        )
+
+        gate = consts.tile([P, B * QT, D], F32)
+        x_grp_of = {}
+        for b in range(B + 1):
+            if b < B:
+                x_sb = x_of.pop(b)
+                x_grp = work.tile([P, QT, P, PACK], BF16, align_bytes=64)
+                for half in range(2):
+                    xT_ps = ps_t.tile([P, 2, 2, P], F32, tag="t")
+                    for j in range(2):
+                        words = x_sb[:, 2 * half + j, :].bitcast(F32)
+                        for u in range(2):
+                            nc.tensor.transpose(xT_ps[:, j, u, :], words[:, u * P : (u + 1) * P], ident_f32[:])
+                    nc.vector.tensor_copy(
+                        out=x_grp[:, 2 * half : 2 * half + 2, :, :]
+                        .rearrange("p j r t -> p (j r t)")
+                        .bitcast(F32)
+                        .rearrange("p (j r u) -> p j r u", j=2, u=2),
+                        in_=xT_ps[:].rearrange("p j u r -> p j r u"),
+                    )
+                x_grp_of[b] = x_grp
+                if b + 3 < B:
+                    x_of[b + 3] = load_x(b + 3)
+            if b >= 1:
+                x_codes = work.tile([P, QT * P], U32, align_bytes=64)
+                x_scales = work.tile([P, QT * P], U8, align_bytes=64)
+                nc.vector.quantize_mx(
+                    out=x_codes[:].bitcast(FP8X4), scales=x_scales[:],
+                    in_=x_grp_of.pop(b - 1)[:].rearrange("p i r t -> p (i r t)"),
+                )
+                for i in range(QT):
+                    rows = slice(i * P, (i + 1) * P)
+                    g_ps = ps_s.tile([P, D], F32, tag="s")
+                    nc.tensor.matmul_mx(
+                        out=g_ps[:],
+                        lhsT=x_codes[:, rows].bitcast(FP8X4), lhsT_scale=x_scales[:, rows],
+                        rhs=w_codes[:].bitcast(FP8X4), rhs_scale=w_scales[:],
+                        start=True, stop=True,
+                    )
+                    nc.scalar.activation(out=gate[:, (b - 1) * QT + i, :], in_=g_ps[:], func=ACT.Silu)
+        qkv_of[1] = load_qkv(1)
+
+        qkT_of, v_grp_of, v_mx_of = {}, {}, {}
+        s_of, bias_of, e_of, sum_of, eT_of, e_mx_of = {}, {}, {}, {}, {}, {}
+        coef_of, y_of, part2_of, diff_of, gated_of, sq_of = {}, {}, {}, {}, {}, {}
+
+        def transpose_qk(b, h):
+            q_sb, k_sb, v_sb = qkv_of[b]
+            feats = slice(h * DH, (h + 1) * DH)
+            qk_ps = ps_t.tile([P, 2, T], BF16, tag="t")
+            for i in range(QT):
+                rows = slice(i * P, (i + 1) * P)
+                nc.tensor.transpose(qk_ps[:, 0, rows], q_sb[:, i, feats], ident_bf[:])
+                nc.tensor.transpose(qk_ps[:, 1, rows], k_sb[:, i, feats], ident_bf[:])
+            qkT_of[(b, h)] = batch.tile([P, 2, T], BF16, name="qkT%d" % h)
+            return qk_ps
+
+        def group_v(b):
+            v_grp_of[b] = batch.tile([P, D, PACK], BF16, name="v_grp", align_bytes=64, bufs=1)
+            interleave_rows(nc, v_grp_of[b][:], qkv_of[b][2][:])
+
+        def quantise_v(b):
+            v_codes = batch.tile([P, D], U32, align_bytes=64)
+            v_scales = batch.tile([P, D], U8, align_bytes=64)
+            nc.vector.quantize_mx(
+                out=v_codes[:].bitcast(FP8X4), scales=v_scales[:],
+                in_=v_grp_of.pop(b)[:].rearrange("p c t -> p (c t)"),
+            )
+            v_mx_of[b] = (v_codes, v_scales)
+
+        def scores(g, h):
+            i = query_tile(g, h // 2)
+            qkT = qkT_of[(g // QT, h)]
+            own = slice(i * P, (i + 1) * P)
+            s_ps = ps_s.tile([P, T], F32, tag="s")
+            if i > 0:
+                nc.tensor.matmul(
+                    out=s_ps[:, 0 : i * P], lhsT=qkT[:, 0, own], rhs=qkT[:, 1, 0 : i * P], start=True, stop=True
+                )
+            nc.tensor.matmul(out=s_ps[:, own], lhsT=qkT[:, 0, own], rhs=qkT[:, 1, own], start=True, stop=False)
+            nc.tensor.matmul(out=s_ps[:, own], lhsT=ident_bf[:], rhs=mask_bf[:], start=False, stop=True)
+            s_of[(g, h)] = s_ps
+
+        def row_max(g, h):
+            n_keys = (query_tile(g, h // 2) + 1) * P
+            if h == 0:
+                bias_of[g] = small.tile([P, H], F32, name="bias")
+            unused = work.tile([P, T], BF16, name="unused")
+            nc.vector.tensor_scalar(
+                out=unused[:, 0:n_keys], in0=s_of[(g, h)][:, 0:n_keys], scalar1=-SCALE, scalar2=None,
+                op0=ALU.mult, op1=ALU.min, accum_out=bias_of[g][:, h : h + 1],
+            )
+
+        def exponent(g, h):
+            n_keys = (query_tile(g, h // 2) + 1) * P
+            if h == 0:
+                e_of[g] = work.tile([P, H, T], BF16, name="e_sb")
+                sum_of[g] = small.tile([P, H], F32, name="row_sum")
+            nc.scalar.activation(
+                out=e_of[g][:, h, 0:n_keys], in_=s_of.pop((g, h))[:, 0:n_keys], func=ACT.Exp,
+                bias=bias_of[g][:, h : h + 1], scale=SCALE, accum_out=sum_of[g][:, h : h + 1],
+            )
+
+        def transpose_e(g, pair):
+            n_tiles = query_tile(g, pair) + 1
+            eT_ps = ps_t.tile([P, 2, PACK, P], BF16, tag="t")
+            for m in range(2):
+                for t in range(n_tiles):
+                    nc.tensor.transpose(
+                        eT_ps[:, m, t, :], e_of[g][:, 2 * pair + m, t * P : (t + 1) * P], ident_bf[:]
+                    )
+            eT_of[(g, pair)] = eT_ps
+
+        def group_e_views(g, pair):
+            n_tiles = query_tile(g, pair) + 1
+            grouped = e_grp[g % QT][:, 2 * pair : 2 * pair + 2, :, 0:n_tiles]
+            planes = eT_of.pop((g, pair))[:, :, 0:n_tiles, :].rearrange("p m t q -> p m q t")
+            return grouped, planes
+
+        def quantise_e(g):
+            e_codes = work.tile([P, H * P], U32, align_bytes=64)
+            e_scales = work.tile([P, H * P], U8, align_bytes=64)
+            nc.vector.quantize_mx(
+                out=e_codes[:].bitcast(FP8X4), scales=e_scales[:],
+                in_=e_grp[g % QT][:].rearrange("p h q t -> p (h q t)"),
+            )
+            e_mx_of[g] = (e_codes, e_scales)
+
+        def coefficients(g):
+            inv_sum = small.tile([P, H], F32)
+            nc.vector.reciprocal(out=inv_sum[:], in_=sum_of.pop(g)[:])
+            coef2 = small.tile([P, HP], F32)
+            nc.vector.tensor_tensor(
+                out=coef2[:], in0=inv_sum[:].rearrange("p (c m) -> p c m", m=2)[:, :, 1], in1=neg_lam[:], op=ALU.mult
+            )
+            coef_of[g] = (inv_sum, coef2)
+
+        def values(g, pair):
+            e_codes, e_scales = e_mx_of[g]
+            v_codes, v_scales = v_mx_of[g // QT]
+            cols = slice(pair * DV, (pair + 1) * DV)
+            y_ps = ps_y.tile([P, 2, DV], F32, tag="y")
+            for m in range(2):
+                qs = slice((2 * pair + m) * P, (2 * pair + m + 1) * P)
+                nc.tensor.matmul_mx(
+                    out=y_ps[:, m, :],
+                    lhsT=e_codes[:, qs].bitcast(FP8X4), lhsT_scale=e_scales[:, qs],
+                    rhs=v_codes[:, cols].bitcast(FP8X4), rhs_scale=v_scales[:, cols],
+                    start=True, stop=True,
+                )
+            y_of[(g, pair)] = y_ps
+
+        def scale_map2(g, pair):
+            if pair == 0:
+                part2_of[g] = tail.tile([P, HP, DV], F32, name="part2")
+            nc.scalar.activation(
+                out=part2_of[g][:, pair, :], in_=y_of[(g, pair)][:, 1, :], func=ACT.Copy,
+                scale=coef_of[g][1][:, pair : pair + 1],
+            )
+
+        def difference(g, pair):
+            if pair == 0:
+                diff_of[g] = tail.tile([P, HP, DV], F32, name="diff")
+            nc.vector.scalar_tensor_tensor(
+                out=diff_of[g][:, pair, :], in0=y_of.pop((g, pair))[:, 0, :],
+                scalar=coef_of[g][0][:, 2 * pair : 2 * pair + 1], in1=part2_of[g][:, pair, :],
+                op0=ALU.mult, op1=ALU.add,
+            )
+
+        def apply_gate(g, pair):
+            if pair == 0:
+                gated_of[g] = tail.tile([P, HP, DV], F32, name="gated")
+            row_tile = (g // QT) * QT + query_tile(g, pair)
+            nc.gpsimd.tensor_tensor(
+                out=gated_of[g][:, pair, :], in0=diff_of[g][:, pair, :],
+                in1=gate[:, row_tile, pair * DV : (pair + 1) * DV], op=ALU.mult,
+            )
+
+        def square_sum(g, pair):
+            if pair == 0:
+                sq_of[g] = small.tile([P, HP], F32, name="sum_sq")
+            squares = work.tile([P, DV], F32, name="squares")
+            nc.scalar.activation(
+                out=squares[:], in_=gated_of[g][:, pair, :], func=ACT.Square, accum_out=sq_of[g][:, pair : pair + 1]
+            )
+
+        def normalise(g):
+            var = small.tile([P, HP], F32)
+            nc.gpsimd.tensor_scalar(
+                out=var[:], in0=sq_of.pop(g)[:], scalar1=1.0 / (DV * (1.0 - LAMBDA_INIT) ** 2),
+                scalar2=EPS / (1.0 - LAMBDA_INIT) ** 2, op0=ALU.mult, op1=ALU.add,
+            )
+            rstd = small.tile([P, HP], F32)
+            nc.gpsimd.tensor_tensor(out=rstd[:], in0=var[:], in1=minus_half[:], op=ALU.pow)
+            out_sb = tail.tile([P, HP, DV], F32)
+            for pair in range(HP):
+                i = query_tile(g, pair)
+                nc.gpsimd.tensor_scalar(
+                    out=out_sb[:, pair, :], in0=gated_of[g][:, pair, :], scalar1=rstd[:, pair : pair + 1],
+                    scalar2=0.0, op0=ALU.mult, op1=ALU.add,
+                )
+                nc.sync.dma_start(
+                    out=out[g // QT, i * P : (i + 1) * P, pair * DV : (pair + 1) * DV], in_=out_sb[:, pair, :]
+                )
+
+        group_v(0)
+        for h in range(H):
+            qk_ps = transpose_qk(0, h)
+            nc.vector.tensor_copy(out=qkT_of[(0, h)][:], in_=qk_ps[:])
+        quantise_v(0)
+
+        for k in range(-1, N_GROUPS + 3):
+            if in_range(k - 1):
+                quantise_e(k - 1)
+                coefficients(k - 1)
+            if in_range(k - 2):
+                for pair in range(HP):
+                    difference(k - 2, pair)
+                    apply_gate(k - 2, pair)
+            for pair in range(HP):
+                if in_range(k):
+                    exponent(k, 2 * pair)
+                    exponent(k, 2 * pair + 1)
+                if in_range(k + 1):
+                    scores(k + 1, 2 * pair)
+                    scores(k + 1, 2 * pair + 1)
+                if in_range(k):
+                    transpose_e(k, pair)
+                    if pair == 0:
+                        grouped, planes = group_e_views(k, 0)
+                        nc.vector.tensor_copy(out=grouped, in_=planes)
+                if in_range(k - 1):
+                    values(k - 1, pair)
+            if in_range(k - 1):
+                scale_map2(k - 1, 0)
+            if in_range(k - 3):
+                square_sum(k - 3, 0)
+                square_sum(k - 3, 1)
+                normalise(k - 3)
+            if in_range(k):
+                grouped, planes = group_e_views(k, 1)
+                nc.scalar.copy(out=grouped, in_=planes)
+            if in_range(k - 1):
+                scale_map2(k - 1, 1)
+            if in_range(k + 5):
+                nb, h = divmod(k + 5, QT)
+                if h == 0 and nb + 1 < B:
+                    qkv_of[nb + 1] = load_qkv(nb + 1)
+                qk_ps = transpose_qk(nb, h)
+                if h % 2 == 0:
+                    nc.vector.tensor_copy(out=qkT_of[(nb, h)][:], in_=qk_ps[:])
+                else:
+                    nc.scalar.copy(out=qkT_of[(nb, h)][:], in_=qk_ps[:])
+                if h == QT - 2:
+                    group_v(nb)
+                if h == QT - 1:
+                    quantise_v(nb)
+            if in_range(k + 1):
+                for h in range(H):
+                    row_max(k + 1, h)

@@ -58,10 +58,12 @@ def tile_mixerdiffattention_pb_t_kernel(
         loads = ctx.enter_context(tc.tile_pool(name="loads", bufs=2))
         batch = ctx.enter_context(tc.tile_pool(name="batch", bufs=2))
         work = ctx.enter_context(tc.tile_pool(name="work", bufs=3))
+        gate_work = ctx.enter_context(tc.tile_pool(name="gate_work", bufs=2))
+        scaled = ctx.enter_context(tc.tile_pool(name="scaled", bufs=6))
         tail = ctx.enter_context(tc.tile_pool(name="tail", bufs=3))
         small = ctx.enter_context(tc.tile_pool(name="small", bufs=6))
-        ps_s = ctx.enter_context(tc.psum_pool(name="ps_s", bufs=4))
-        ps_t = ctx.enter_context(tc.psum_pool(name="ps_t", bufs=2))
+        ps_s = ctx.enter_context(tc.psum_pool(name="ps_s", bufs=3))
+        ps_t = ctx.enter_context(tc.psum_pool(name="ps_t", bufs=3))
         ps_y = ctx.enter_context(tc.psum_pool(name="ps_y", bufs=2))
 
         def load_x(b):
@@ -134,12 +136,12 @@ def tile_mixerdiffattention_pb_t_kernel(
             op0=ALU.add, op1=ALU.subtract,
         )
 
-        gate = consts.tile([P, B * QT, D], F32)
+        gate = consts.tile([P, N_GROUPS, HP, DV], F32)
         x_grp_of = {}
         for b in range(B + 1):
             if b < B:
                 x_sb = x_of.pop(b)
-                x_grp = work.tile([P, QT, P, PACK], BF16, align_bytes=64)
+                x_grp = gate_work.tile([P, QT, P, PACK], BF16, align_bytes=64)
                 for half in range(2):
                     xT_ps = ps_t.tile([P, 2, 2, P], F32, tag="t")
                     for j in range(2):
@@ -157,8 +159,8 @@ def tile_mixerdiffattention_pb_t_kernel(
                 if b + 3 < B:
                     x_of[b + 3] = load_x(b + 3)
             if b >= 1:
-                x_codes = work.tile([P, QT * P], U32, align_bytes=64)
-                x_scales = work.tile([P, QT * P], U8, align_bytes=64)
+                x_codes = gate_work.tile([P, QT * P], U32, align_bytes=64)
+                x_scales = gate_work.tile([P, QT * P], U8, align_bytes=64)
                 nc.vector.quantize_mx(
                     out=x_codes[:].bitcast(FP8X4), scales=x_scales[:],
                     in_=x_grp_of.pop(b - 1)[:].rearrange("p i r t -> p (i r t)"),
@@ -172,10 +174,14 @@ def tile_mixerdiffattention_pb_t_kernel(
                         rhs=w_codes[:].bitcast(FP8X4), rhs_scale=w_scales[:],
                         start=True, stop=True,
                     )
-                    nc.scalar.activation(out=gate[:, (b - 1) * QT + i, :], in_=g_ps[:], func=ACT.Silu)
+                    nc.scalar.activation(out=gate[:, (b - 1) * QT + i, 0, :], in_=g_ps[:, 0:DV], func=ACT.Silu)
+                    nc.scalar.activation(
+                        out=gate[:, (b - 1) * QT + QT - 1 - i, 1, :], in_=g_ps[:, DV:D], func=ACT.Silu
+                    )
         qkv_of[1] = load_qkv(1)
 
         qkT_of, v_grp_of, v_mx_of = {}, {}, {}
+        neg_s_of = {}
         s_of, bias_of, e_of, sum_of, eT_of, e_mx_of = {}, {}, {}, {}, {}, {}
         coef_of, y_of, part2_of, diff_of, gated_of, sq_of = {}, {}, {}, {}, {}, {}
 
@@ -220,11 +226,12 @@ def tile_mixerdiffattention_pb_t_kernel(
             n_keys = (query_tile(g, h // 2) + 1) * P
             if h == 0:
                 bias_of[g] = small.tile([P, H], F32, name="bias")
-            unused = work.tile([P, T], BF16, name="unused")
+            neg_s = scaled.tile([P, T], F32, name="neg_s")
             nc.vector.tensor_scalar(
-                out=unused[:, 0:n_keys], in0=s_of[(g, h)][:, 0:n_keys], scalar1=-SCALE, scalar2=None,
+                out=neg_s[:, 0:n_keys], in0=s_of.pop((g, h))[:, 0:n_keys], scalar1=-SCALE, scalar2=None,
                 op0=ALU.mult, op1=ALU.min, accum_out=bias_of[g][:, h : h + 1],
             )
+            neg_s_of[(g, h)] = neg_s
 
         def exponent(g, h):
             n_keys = (query_tile(g, h // 2) + 1) * P
@@ -232,8 +239,8 @@ def tile_mixerdiffattention_pb_t_kernel(
                 e_of[g] = work.tile([P, H, T], BF16, name="e_sb")
                 sum_of[g] = small.tile([P, H], F32, name="row_sum")
             nc.scalar.activation(
-                out=e_of[g][:, h, 0:n_keys], in_=s_of.pop((g, h))[:, 0:n_keys], func=ACT.Exp,
-                bias=bias_of[g][:, h : h + 1], scale=SCALE, accum_out=sum_of[g][:, h : h + 1],
+                out=e_of[g][:, h, 0:n_keys], in_=neg_s_of.pop((g, h))[:, 0:n_keys], func=ACT.Exp,
+                bias=bias_of[g][:, h : h + 1], scale=-1.0, accum_out=sum_of[g][:, h : h + 1],
             )
 
         def transpose_e(g, pair):
@@ -302,19 +309,14 @@ def tile_mixerdiffattention_pb_t_kernel(
                 op0=ALU.mult, op1=ALU.add,
             )
 
-        def apply_gate(g, pair):
-            if pair == 0:
-                gated_of[g] = tail.tile([P, HP, DV], F32, name="gated")
-            row_tile = (g // QT) * QT + query_tile(g, pair)
-            nc.gpsimd.tensor_tensor(
-                out=gated_of[g][:, pair, :], in0=diff_of[g][:, pair, :],
-                in1=gate[:, row_tile, pair * DV : (pair + 1) * DV], op=ALU.mult,
-            )
+        def apply_gate(g):
+            gated_of[g] = tail.tile([P, HP, DV], F32, name="gated")
+            nc.gpsimd.tensor_tensor(out=gated_of[g][:], in0=diff_of[g][:], in1=gate[:, g, :, :], op=ALU.mult)
 
         def square_sum(g, pair):
             if pair == 0:
                 sq_of[g] = small.tile([P, HP], F32, name="sum_sq")
-            squares = work.tile([P, DV], F32, name="squares")
+            squares = work.tile([P, DV], F32, name="squares", bufs=2)
             nc.scalar.activation(
                 out=squares[:], in_=gated_of[g][:, pair, :], func=ACT.Square, accum_out=sq_of[g][:, pair : pair + 1]
             )
@@ -351,7 +353,7 @@ def tile_mixerdiffattention_pb_t_kernel(
             if in_range(k - 2):
                 for pair in range(HP):
                     difference(k - 2, pair)
-                    apply_gate(k - 2, pair)
+                apply_gate(k - 2)
             for pair in range(HP):
                 if in_range(k):
                     exponent(k, 2 * pair)

@@ -77,7 +77,10 @@ def tile_mixerdiffattention_pb_t_kernel(
             v_sb = loads.tile([P, PACK, D], BF16, name="v_sb")
             nc.sync.dma_start(out=q_sb[:], in_=q_rot[b].rearrange("(i p) h d -> p i (h d)", p=P))
             nc.sync.dma_start(out=k_sb[:], in_=k_rot[b].rearrange("(i p) h d -> p i (h d)", p=P))
-            nc.sync.dma_start(out=v_sb[:], in_=v[b].rearrange("(t p) h c -> p t (h c)", p=P))
+            nc.sync.dma_start(
+                out=v_sb[:].rearrange("p (u e) n -> p u (e n)", u=2),
+                in_=v[b].rearrange("(u p e) h c -> p u (e h c)", u=2, e=2),
+            )
             return q_sb, k_sb, v_sb
 
         w_sb = consts.tile([P, PACK, D], BF16)
@@ -108,9 +111,9 @@ def tile_mixerdiffattention_pb_t_kernel(
         )
         minus_half = consts.tile([P, HP], F32)
         nc.vector.memset(minus_half[:], -0.5)
-        e_grp = [consts.tile([P, H, P, PACK], BF16, name="e_grp%d" % j, align_bytes=64) for j in range(QT)]
+        e_sb = [consts.tile([P, H, T], BF16, name="e_sb%d" % j) for j in range(QT)]
         for j in range(QT):
-            nc.gpsimd.memset(e_grp[j][:], 0.0)
+            nc.gpsimd.memset(e_sb[j][:], 0.0)
 
         w_grp = consts.tile([P, D, PACK], BF16, align_bytes=64)
         interleave_rows(nc, w_grp[:], w_sb[:])
@@ -181,7 +184,7 @@ def tile_mixerdiffattention_pb_t_kernel(
         qkv_of[1] = load_qkv(1)
 
         qkT_of, v_grp_of, v_mx_of = {}, {}, {}
-        neg_s_of = {}
+        neg_s_of, e_grp_of = {}, {}
         s_of, bias_of, e_of, sum_of, eT_of, e_mx_of = {}, {}, {}, {}, {}, {}
         coef_of, y_of, part2_of, diff_of, gated_of, sq_of = {}, {}, {}, {}, {}, {}
 
@@ -236,7 +239,7 @@ def tile_mixerdiffattention_pb_t_kernel(
         def exponent(g, h):
             n_keys = (query_tile(g, h // 2) + 1) * P
             if h == 0:
-                e_of[g] = work.tile([P, H, T], BF16, name="e_sb")
+                e_of[g] = e_sb[g % QT]
                 sum_of[g] = small.tile([P, H], F32, name="row_sum")
             nc.scalar.activation(
                 out=e_of[g][:, h, 0:n_keys], in_=neg_s_of.pop((g, h))[:, 0:n_keys], func=ACT.Exp,
@@ -244,19 +247,23 @@ def tile_mixerdiffattention_pb_t_kernel(
             )
 
         def transpose_e(g, pair):
-            n_tiles = query_tile(g, pair) + 1
-            eT_ps = ps_t.tile([P, 2, PACK, P], BF16, tag="t")
+            eT_ps = ps_t.tile([P, 2, 2, P], F32, tag="t")
             for m in range(2):
-                for t in range(n_tiles):
-                    nc.tensor.transpose(
-                        eT_ps[:, m, t, :], e_of[g][:, 2 * pair + m, t * P : (t + 1) * P], ident_bf[:]
-                    )
+                words = e_of[g][:, 2 * pair + m, :].bitcast(F32)
+                for u in range(2):
+                    nc.tensor.transpose(eT_ps[:, m, u, :], words[:, u * P : (u + 1) * P], ident_f32[:])
             eT_of[(g, pair)] = eT_ps
 
         def group_e_views(g, pair):
-            n_tiles = query_tile(g, pair) + 1
-            grouped = e_grp[g % QT][:, 2 * pair : 2 * pair + 2, :, 0:n_tiles]
-            planes = eT_of.pop((g, pair))[:, :, 0:n_tiles, :].rearrange("p m t q -> p m q t")
+            if pair == 0:
+                e_grp_of[g] = work.tile([P, H, P, PACK], BF16, name="e_grp", align_bytes=64)
+            grouped = (
+                e_grp_of[g][:, 2 * pair : 2 * pair + 2, :, :]
+                .rearrange("p m q t -> p (m q t)")
+                .bitcast(F32)
+                .rearrange("p (m q u) -> p m q u", m=2, u=2)
+            )
+            planes = eT_of.pop((g, pair))[:].rearrange("p m u q -> p m q u")
             return grouped, planes
 
         def quantise_e(g):
@@ -264,7 +271,7 @@ def tile_mixerdiffattention_pb_t_kernel(
             e_scales = work.tile([P, H * P], U8, align_bytes=64)
             nc.vector.quantize_mx(
                 out=e_codes[:].bitcast(FP8X4), scales=e_scales[:],
-                in_=e_grp[g % QT][:].rearrange("p h q t -> p (h q t)"),
+                in_=e_grp_of.pop(g)[:].rearrange("p h q t -> p (h q t)"),
             )
             e_mx_of[g] = (e_codes, e_scales)
 

@@ -28,6 +28,7 @@ SCALE = DH ** -0.5
 MASKED = -1e30
 
 N_GROUPS = B * QT
+DRAIN = 3
 assert H == QT
 
 FLOPS = 2 * B * H * T * T * DH + 2 * B * H * T * T * DV + 2 * B * T * D * D
@@ -139,7 +140,7 @@ def tile_mixerdiffattention_pb_t_kernel(
             op0=ALU.add, op1=ALU.subtract,
         )
 
-        gate = consts.tile([P, N_GROUPS, HP, DV], F32)
+        gate = consts.tile([P, B, HP, QT, DV], F32)
         x_grp_of = {}
         for b in range(B + 1):
             if b < B:
@@ -177,9 +178,11 @@ def tile_mixerdiffattention_pb_t_kernel(
                         rhs=w_codes[:].bitcast(FP8X4), rhs_scale=w_scales[:],
                         start=True, stop=True,
                     )
-                    nc.scalar.activation(out=gate[:, (b - 1) * QT + i, 0, :], in_=g_ps[:, 0:DV], func=ACT.Silu)
                     nc.scalar.activation(
-                        out=gate[:, (b - 1) * QT + QT - 1 - i, 1, :], in_=g_ps[:, DV:D], func=ACT.Silu
+                        out=gate[:, b - 1, :, :, :].rearrange("p c j n -> p (c j) n")[
+                            :, i : 2 * QT - i : 2 * QT - 1 - 2 * i, :
+                        ],
+                        in_=g_ps[:].rearrange("p (c n) -> p c n", c=HP), func=ACT.Silu,
                     )
         qkv_of[1] = load_qkv(1)
 
@@ -318,7 +321,8 @@ def tile_mixerdiffattention_pb_t_kernel(
 
         def apply_gate(g):
             gated_of[g] = tail.tile([P, HP, DV], F32, name="gated")
-            nc.gpsimd.tensor_tensor(out=gated_of[g][:], in0=diff_of[g][:], in1=gate[:, g, :, :], op=ALU.mult)
+            engine = nc.vector if g >= N_GROUPS - DRAIN else nc.gpsimd
+            engine.tensor_tensor(out=gated_of[g][:], in0=diff_of[g][:], in1=gate[:, g // QT, :, g % QT, :], op=ALU.mult)
 
         def square_sum(g, pair):
             if pair == 0:
@@ -337,9 +341,10 @@ def tile_mixerdiffattention_pb_t_kernel(
             rstd = small.tile([P, HP], F32)
             nc.gpsimd.tensor_tensor(out=rstd[:], in0=var[:], in1=minus_half[:], op=ALU.pow)
             out_sb = tail.tile([P, HP, DV], F32)
+            engine = nc.vector if g >= N_GROUPS - DRAIN else nc.gpsimd
             for pair in range(HP):
                 i = query_tile(g, pair)
-                nc.gpsimd.tensor_scalar(
+                engine.tensor_scalar(
                     out=out_sb[:, pair, :], in0=gated_of[g][:, pair, :], scalar1=rstd[:, pair : pair + 1],
                     scalar2=0.0, op0=ALU.mult, op1=ALU.add,
                 )

@@ -112,6 +112,12 @@ def tile_mixerdiffattention_pb_t_kernel(
         )
         minus_half = consts.tile([P, HP], F32)
         nc.vector.memset(minus_half[:], -0.5)
+        gated_sb = [consts.tile([P, HP, DV + 8], F32, name="gated_sb%d" % r) for r in range(3)]
+        for r in range(3):
+            nc.vector.tensor_scalar(
+                out=gated_sb[r][:, :, DV], in0=minus_half[:], scalar1=0.0, scalar2=math.sqrt(EPS * DV),
+                op0=ALU.mult, op1=ALU.add,
+            )
         e_sb = [consts.tile([P, H, T], BF16, name="e_sb%d" % j) for j in range(QT)]
         for j in range(QT):
             nc.gpsimd.memset(e_sb[j][:], 0.0)
@@ -320,32 +326,30 @@ def tile_mixerdiffattention_pb_t_kernel(
             )
 
         def apply_gate(g):
-            gated_of[g] = tail.tile([P, HP, DV], F32, name="gated")
+            gated_of[g] = gated_sb[g % len(gated_sb)]
             engine = nc.vector if g >= N_GROUPS - DRAIN else nc.gpsimd
-            engine.tensor_tensor(out=gated_of[g][:], in0=diff_of[g][:], in1=gate[:, g // QT, :, g % QT, :], op=ALU.mult)
+            engine.tensor_tensor(
+                out=gated_of[g][:, :, 0:DV], in0=diff_of[g][:], in1=gate[:, g // QT, :, g % QT, :], op=ALU.mult
+            )
 
         def square_sum(g, pair):
             if pair == 0:
                 sq_of[g] = small.tile([P, HP], F32, name="sum_sq")
-            squares = work.tile([P, DV], F32, name="squares", bufs=2)
+            squares = work.tile([P, DV + 1], F32, name="squares", bufs=2)
             nc.scalar.activation(
-                out=squares[:], in_=gated_of[g][:, pair, :], func=ACT.Square, accum_out=sq_of[g][:, pair : pair + 1]
+                out=squares[:], in_=gated_of[g][:, pair, 0 : DV + 1], func=ACT.Square,
+                scale=1.0 / (math.sqrt(DV) * (1.0 - LAMBDA_INIT)), accum_out=sq_of[g][:, pair : pair + 1],
             )
 
         def normalise(g):
-            var = small.tile([P, HP], F32)
-            nc.gpsimd.tensor_scalar(
-                out=var[:], in0=sq_of.pop(g)[:], scalar1=1.0 / (DV * (1.0 - LAMBDA_INIT) ** 2),
-                scalar2=EPS / (1.0 - LAMBDA_INIT) ** 2, op0=ALU.mult, op1=ALU.add,
-            )
             rstd = small.tile([P, HP], F32)
-            nc.gpsimd.tensor_tensor(out=rstd[:], in0=var[:], in1=minus_half[:], op=ALU.pow)
+            nc.gpsimd.tensor_tensor(out=rstd[:], in0=sq_of.pop(g)[:], in1=minus_half[:], op=ALU.pow)
             out_sb = tail.tile([P, HP, DV], F32)
             engine = nc.vector if g >= N_GROUPS - DRAIN else nc.gpsimd
             for pair in range(HP):
                 i = query_tile(g, pair)
                 engine.tensor_scalar(
-                    out=out_sb[:, pair, :], in0=gated_of[g][:, pair, :], scalar1=rstd[:, pair : pair + 1],
+                    out=out_sb[:, pair, :], in0=gated_of[g][:, pair, 0:DV], scalar1=rstd[:, pair : pair + 1],
                     scalar2=0.0, op0=ALU.mult, op1=ALU.add,
                 )
                 nc.sync.dma_start(

@@ -400,7 +400,7 @@ def tile_mixerdiffattention_pb_t_kernel(
                 if h == 0 and nb + 1 < B:
                     qkv_of[nb + 1] = load_qkv(nb + 1)
                 qk_ps = transpose_qk(nb, h)
-                if h % 2 == 0:
+                if h == 0 or (h == 2 and nb % 2 == 0):
                     nc.vector.tensor_copy(out=qkT_of[(nb, h)][:], in_=qk_ps[:])
                 else:
                     nc.scalar.copy(out=qkT_of[(nb, h)][:], in_=qk_ps[:])

import math
from contextlib import ExitStack

import concourse.mybir as mybir
from concourse.masks import make_identity

F32 = mybir.dt.float32
BF16 = mybir.dt.bfloat16
U32 = mybir.dt.uint32
U8 = mybir.dt.uint8
FP8X4 = mybir.dt.float8_e4m3fn_x4
ACT = mybir.ActivationFunctionType
ALU = mybir.AluOpType
AX = mybir.AxisListType

B, T, D, H = 8, 512, 512, 4
DH = D // H
HP = H // 2
DV = 2 * DH
P = 128
PACK = 4
QT = T // P
LAM_LEN = DH // 2

EPS = 1e-6
LAMBDA_INIT = 0.8 - 0.6 * math.exp(-0.3 * 6)
SCALE = DH ** -0.5
MASKED = -1e30

N_GROUPS = B * QT
DRAIN = 3
assert H == QT

FLOPS = 2 * B * H * T * T * DH + 2 * B * H * T * T * DV + 2 * B * T * D * D


def interleave_rows(nc, grouped, rows):
    nc.vector.tensor_copy(
        out=grouped.rearrange("p (c i) t -> p c t i", i=4),
        in_=rows.rearrange("p t (c i) -> p c t i", i=4),
    )


def in_range(g):
    return 0 <= g < N_GROUPS


def query_tile(g, pair):
    j = g % QT
    return j if pair == 0 else QT - 1 - j


def tile_mixerdiffattention_pb_t_kernel(
    tc, q_rot, k_rot, v, hidden_states, W_g, lambda_q1, lambda_k1, lambda_q2, lambda_k2, out
):
    nc = tc.nc
    with ExitStack() as ctx:
        consts = ctx.enter_context(tc.tile_pool(name="consts", bufs=1))
        loads = ctx.enter_context(tc.tile_pool(name="loads", bufs=2))
        batch = ctx.enter_context(tc.tile_pool(name="batch", bufs=2))
        work = ctx.enter_context(tc.tile_pool(name="work", bufs=3))
        gate_work = ctx.enter_context(tc.tile_pool(name="gate_work", bufs=2))
        scaled = ctx.enter_context(tc.tile_pool(name="scaled", bufs=6))
        tail = ctx.enter_context(tc.tile_pool(name="tail", bufs=3))
        small = ctx.enter_context(tc.tile_pool(name="small", bufs=6))
        ps_s = ctx.enter_context(tc.psum_pool(name="ps_s", bufs=3))
        ps_t = ctx.enter_context(tc.psum_pool(name="ps_t", bufs=3))
        ps_y = ctx.enter_context(tc.psum_pool(name="ps_y", bufs=2))

        def load_x(b):
            x_sb = loads.tile([P, QT, D], BF16, name="x_sb", bufs=3)
            nc.sync.dma_start(out=x_sb[:], in_=hidden_states[b].rearrange("(i p) k -> p i k", p=P))
            return x_sb

        def load_qkv(b):
            q_sb = loads.tile([P, QT, D], BF16, name="q_sb")
            k_sb = loads.tile([P, QT, D], BF16, name="k_sb")
            v_sb = loads.tile([P, PACK, D], BF16, name="v_sb")
            nc.sync.dma_start(out=q_sb[:], in_=q_rot[b].rearrange("(i p) h d -> p i (h d)", p=P))
            nc.sync.dma_start(out=k_sb[:], in_=k_rot[b].rearrange("(i p) h d -> p i (h d)", p=P))
            nc.sync.dma_start(
                out=v_sb[:].rearrange("p (u e) n -> p u (e n)", u=2),
                in_=v[b].rearrange("(u p e) h c -> p u (e h c)", u=2, e=2),
            )
            return q_sb, k_sb, v_sb

        w_sb = consts.tile([P, PACK, D], BF16)
        nc.sync.dma_start(
            out=w_sb[:].rearrange("p (u e) n -> p u (e n)", u=2),
            in_=W_g.rearrange("(u p e) n -> p u (e n)", u=2, e=2),
        )
        x_of = {0: load_x(0)}
        lam_in = consts.tile([P, 2, 2, HP * LAM_LEN], BF16)
        for j, vec in enumerate((lambda_q1, lambda_k1, lambda_q2, lambda_k2)):
            nc.sync.dma_start(
                out=lam_in[:, j // 2, j % 2, :],
                in_=vec.rearrange("h j -> (h j)").partition_broadcast(P),
            )
        x_of[1] = load_x(1)
        x_of[2] = load_x(2)
        qkv_of = {0: load_qkv(0)}

        ident_f32 = consts.tile([P, P], F32)
        make_identity(nc, ident_f32[:])
        ident_bf = consts.tile([P, P], BF16)
        make_identity(nc, ident_bf[:])
        mask_f32 = consts.tile([P, P], F32)
        nc.gpsimd.memset(mask_f32[:], 0.0)
        nc.gpsimd.affine_select(
            out=mask_f32[:], in_=mask_f32[:], pattern=[[-1, P]], compare_op=ALU.is_ge,
            fill=MASKED, base=0, channel_multiplier=1,
        )
        minus_half = consts.tile([P, HP], F32)
        nc.vector.memset(minus_half[:], -0.5)
        gated_sb = [consts.tile([P, HP, DV + 8], F32, name="gated_sb%d" % r) for r in range(3)]
        for r in range(3):
            nc.vector.tensor_scalar(
                out=gated_sb[r][:, :, DV], in0=minus_half[:], scalar1=0.0, scalar2=math.sqrt(EPS * DV),
                op0=ALU.mult, op1=ALU.add,
            )
        e_sb = [consts.tile([P, H, T], BF16, name="e_sb%d" % j) for j in range(QT)]
        for j in range(QT):
            nc.gpsimd.memset(e_sb[j][:], 0.0)

        w_grp = consts.tile([P, D, PACK], BF16, align_bytes=64)
        interleave_rows(nc, w_grp[:], w_sb[:])
        mask_bf = consts.tile([P, P], BF16)
        nc.vector.tensor_copy(out=mask_bf[:], in_=mask_f32[:])
        w_codes = consts.tile([P, D], U32, align_bytes=64)
        w_scales = consts.tile([P, D], U8, align_bytes=64)
        nc.vector.quantize_mx(
            out=w_codes[:].bitcast(FP8X4), scales=w_scales[:], in_=w_grp[:].rearrange("p n t -> p (n t)")
        )

        lam_prod = consts.tile([P, 2, HP * LAM_LEN], F32)
        nc.vector.tensor_tensor(out=lam_prod[:], in0=lam_in[:, :, 0, :], in1=lam_in[:, :, 1, :], op=ALU.mult)
        lam_dot = consts.tile([P, 2 * HP], F32)
        nc.vector.tensor_reduce(
            out=lam_dot[:], in_=lam_prod[:].rearrange("p s (h j) -> p (s h) j", h=HP), axis=AX.X, op=ALU.add
        )
        lam_exp = consts.tile([P, 2 * HP], F32)
        nc.scalar.activation(out=lam_exp[:], in_=lam_dot[:], func=ACT.Exp)
        neg_lam = consts.tile([P, HP], F32)
        nc.vector.scalar_tensor_tensor(
            out=neg_lam[:], in0=lam_exp[:, HP : 2 * HP], scalar=-LAMBDA_INIT, in1=lam_exp[:, 0:HP],
            op0=ALU.add, op1=ALU.subtract,
        )

        gate = consts.tile([P, B, HP, QT, DV], F32)
        x_grp_of = {}
        for b in range(B + 1):
            if b < B:
                x_sb = x_of.pop(b)
                x_grp = gate_work.tile([P, QT, P, PACK], BF16, align_bytes=64)
                for half in range(2):
                    xT_ps = ps_t.tile([P, 2, 2, P], F32, tag="t")
                    for j in range(2):
                        words = x_sb[:, 2 * half + j, :].bitcast(F32)
                        for u in range(2):
                            nc.tensor.transpose(xT_ps[:, j, u, :], words[:, u * P : (u + 1) * P], ident_f32[:])
                    nc.vector.tensor_copy(
                        out=x_grp[:, 2 * half : 2 * half + 2, :, :]
                        .rearrange("p j r t -> p (j r t)")
                        .bitcast(F32)
                        .rearrange("p (j r u) -> p j r u", j=2, u=2),
                        in_=xT_ps[:].rearrange("p j u r -> p j r u"),
                    )
                x_grp_of[b] = x_grp
                if b + 3 < B:
                    x_of[b + 3] = load_x(b + 3)
            if b >= 1:
                x_codes = gate_work.tile([P, QT * P], U32, align_bytes=64)
                x_scales = gate_work.tile([P, QT * P], U8, align_bytes=64)
                nc.vector.quantize_mx(
                    out=x_codes[:].bitcast(FP8X4), scales=x_scales[:],
                    in_=x_grp_of.pop(b - 1)[:].rearrange("p i r t -> p (i r t)"),
                )
                for i in range(QT):
                    rows = slice(i * P, (i + 1) * P)
                    g_ps = ps_s.tile([P, D], F32, tag="s")
                    nc.tensor.matmul_mx(
                        out=g_ps[:],
                        lhsT=x_codes[:, rows].bitcast(FP8X4), lhsT_scale=x_scales[:, rows],
                        rhs=w_codes[:].bitcast(FP8X4), rhs_scale=w_scales[:],
                        start=True, stop=True,
                    )
                    nc.scalar.activation(
                        out=gate[:, b - 1, :, :, :].rearrange("p c j n -> p (c j) n")[
                            :, i : 2 * QT - i : 2 * QT - 1 - 2 * i, :
                        ],
                        in_=g_ps[:].rearrange("p (c n) -> p c n", c=HP), func=ACT.Silu,
                    )
        qkv_of[1] = load_qkv(1)

        qkT_of, v_grp_of, v_mx_of = {}, {}, {}
        neg_s_of, e_grp_of = {}, {}
        s_of, bias_of, e_of, sum_of, eT_of, e_mx_of = {}, {}, {}, {}, {}, {}
        coef_of, y_of, part2_of, diff_of, gated_of, sq_of = {}, {}, {}, {}, {}, {}

        def transpose_qk(b, h):
            q_sb, k_sb, v_sb = qkv_of[b]
            feats = slice(h * DH, (h + 1) * DH)
            qk_ps = ps_t.tile([P, 2, T], BF16, tag="t")
            for i in range(QT):
                rows = slice(i * P, (i + 1) * P)
                nc.tensor.transpose(qk_ps[:, 0, rows], q_sb[:, i, feats], ident_bf[:])
                nc.tensor.transpose(qk_ps[:, 1, rows], k_sb[:, i, feats], ident_bf[:])
            qkT_of[(b, h)] = batch.tile([P, 2, T], BF16, name="qkT%d" % h)
            return qk_ps

        def group_v(b):
            v_grp_of[b] = batch.tile([P, D, PACK], BF16, name="v_grp", align_bytes=64, bufs=1)
            interleave_rows(nc, v_grp_of[b][:], qkv_of[b][2][:])

        def quantise_v(b):
            v_codes = batch.tile([P, D], U32, align_bytes=64)
            v_scales = batch.tile([P, D], U8, align_bytes=64)
            nc.vector.quantize_mx(
                out=v_codes[:].bitcast(FP8X4), scales=v_scales[:],
                in_=v_grp_of.pop(b)[:].rearrange("p c t -> p (c t)"),
            )
            v_mx_of[b] = (v_codes, v_scales)

        def scores(g, h):
            i = query_tile(g, h // 2)
            qkT = qkT_of[(g // QT, h)]
            own = slice(i * P, (i + 1) * P)
            s_ps = ps_s.tile([P, T], F32, tag="s")
            if i > 0:
                nc.tensor.matmul(
                    out=s_ps[:, 0 : i * P], lhsT=qkT[:, 0, own], rhs=qkT[:, 1, 0 : i * P], start=True, stop=True
                )
            nc.tensor.matmul(out=s_ps[:, own], lhsT=qkT[:, 0, own], rhs=qkT[:, 1, own], start=True, stop=False)
            nc.tensor.matmul(out=s_ps[:, own], lhsT=ident_bf[:], rhs=mask_bf[:], start=False, stop=True)
            s_of[(g, h)] = s_ps

        def row_max(g, h):
            n_keys = (query_tile(g, h // 2) + 1) * P
            if h == 0:
                bias_of[g] = small.tile([P, H], F32, name="bias")
            neg_s = scaled.tile([P, T], F32, name="neg_s")
            nc.vector.tensor_scalar(
                out=neg_s[:, 0:n_keys], in0=s_of.pop((g, h))[:, 0:n_keys], scalar1=-SCALE, scalar2=None,
                op0=ALU.mult, op1=ALU.min, accum_out=bias_of[g][:, h : h + 1],
            )
            neg_s_of[(g, h)] = neg_s

        def exponent(g, h):
            n_keys = (query_tile(g, h // 2) + 1) * P
            if h == 0:
                e_of[g] = e_sb[g % QT]
                sum_of[g] = small.tile([P, H], F32, name="row_sum")
            nc.scalar.activation(
                out=e_of[g][:, h, 0:n_keys], in_=neg_s_of.pop((g, h))[:, 0:n_keys], func=ACT.Exp,
                bias=bias_of[g][:, h : h + 1], scale=-1.0, accum_out=sum_of[g][:, h : h + 1],
            )

        def transpose_e(g, pair):
            eT_ps = ps_t.tile([P, 2, 2, P], F32, tag="t")
            for m in range(2):
                words = e_of[g][:, 2 * pair + m, :].bitcast(F32)
                for u in range(2):
                    nc.tensor.transpose(eT_ps[:, m, u, :], words[:, u * P : (u + 1) * P], ident_f32[:])
            eT_of[(g, pair)] = eT_ps

        def group_e_views(g, pair):
            if pair == 0:
                e_grp_of[g] = work.tile([P, H, P, PACK], BF16, name="e_grp", align_bytes=64)
            grouped = (
                e_grp_of[g][:, 2 * pair : 2 * pair + 2, :, :]
                .rearrange("p m q t -> p (m q t)")
                .bitcast(F32)
                .rearrange("p (m q u) -> p m q u", m=2, u=2)
            )
            planes = eT_of.pop((g, pair))[:].rearrange("p m u q -> p m q u")
            return grouped, planes

        def quantise_e(g):
            e_codes = work.tile([P, H * P], U32, align_bytes=64)
            e_scales = work.tile([P, H * P], U8, align_bytes=64)
            nc.vector.quantize_mx(
                out=e_codes[:].bitcast(FP8X4), scales=e_scales[:],
                in_=e_grp_of.pop(g)[:].rearrange("p h q t -> p (h q t)"),
            )
            e_mx_of[g] = (e_codes, e_scales)

        def coefficients(g):
            inv_sum = small.tile([P, H], F32)
            nc.vector.reciprocal(out=inv_sum[:], in_=sum_of.pop(g)[:])
            coef2 = small.tile([P, HP], F32)
            nc.vector.tensor_tensor(
                out=coef2[:], in0=inv_sum[:].rearrange("p (c m) -> p c m", m=2)[:, :, 1], in1=neg_lam[:], op=ALU.mult
            )
            coef_of[g] = (inv_sum, coef2)

        def values(g, pair):
            e_codes, e_scales = e_mx_of[g]
            v_codes, v_scales = v_mx_of[g // QT]
            cols = slice(pair * DV, (pair + 1) * DV)
            y_ps = ps_y.tile([P, 2, DV], F32, tag="y")
            for m in range(2):
                qs = slice((2 * pair + m) * P, (2 * pair + m + 1) * P)
                nc.tensor.matmul_mx(
                    out=y_ps[:, m, :],
                    lhsT=e_codes[:, qs].bitcast(FP8X4), lhsT_scale=e_scales[:, qs],
                    rhs=v_codes[:, cols].bitcast(FP8X4), rhs_scale=v_scales[:, cols],
                    start=True, stop=True,
                )
            y_of[(g, pair)] = y_ps

        def scale_map2(g, pair):
            if pair == 0:
                part2_of[g] = tail.tile([P, HP, DV], F32, name="part2")
            nc.scalar.activation(
                out=part2_of[g][:, pair, :], in_=y_of[(g, pair)][:, 1, :], func=ACT.Copy,
                scale=coef_of[g][1][:, pair : pair + 1],
            )

        def difference(g, pair):
            if pair == 0:
                diff_of[g] = tail.tile([P, HP, DV], F32, name="diff")
            nc.vector.scalar_tensor_tensor(
                out=diff_of[g][:, pair, :], in0=y_of.pop((g, pair))[:, 0, :],
                scalar=coef_of[g][0][:, 2 * pair : 2 * pair + 1], in1=part2_of[g][:, pair, :],
                op0=ALU.mult, op1=ALU.add,
            )

        def apply_gate(g):
            gated_of[g] = gated_sb[g % len(gated_sb)]
            engine = nc.vector if g >= N_GROUPS - DRAIN else nc.gpsimd
            engine.tensor_tensor(
                out=gated_of[g][:, :, 0:DV], in0=diff_of[g][:], in1=gate[:, g // QT, :, g % QT, :], op=ALU.mult
            )

        def square_sum(g, pair):
            if pair == 0:
                sq_of[g] = small.tile([P, HP], F32, name="sum_sq")
            squares = work.tile([P, DV + 1], F32, name="squares", bufs=2)
            nc.scalar.activation(
                out=squares[:], in_=gated_of[g][:, pair, 0 : DV + 1], func=ACT.Square,
                scale=1.0 / (math.sqrt(DV) * (1.0 - LAMBDA_INIT)), accum_out=sq_of[g][:, pair : pair + 1],
            )

        def normalise(g):
            rstd = small.tile([P, HP], F32)
            nc.gpsimd.tensor_tensor(out=rstd[:], in0=sq_of.pop(g)[:], in1=minus_half[:], op=ALU.pow)
            out_sb = tail.tile([P, HP, DV], F32)
            engine = nc.vector if g >= N_GROUPS - DRAIN else nc.gpsimd
            for pair in range(HP):
                i = query_tile(g, pair)
                engine.tensor_scalar(
                    out=out_sb[:, pair, :], in0=gated_of[g][:, pair, 0:DV], scalar1=rstd[:, pair : pair + 1],
                    scalar2=0.0, op0=ALU.mult, op1=ALU.add,
                )
                nc.sync.dma_start(
                    out=out[g // QT, i * P : (i + 1) * P, pair * DV : (pair + 1) * DV], in_=out_sb[:, pair, :]
                )

        group_v(0)
        for h in range(H):
            qk_ps = transpose_qk(0, h)
            nc.vector.tensor_copy(out=qkT_of[(0, h)][:], in_=qk_ps[:])
        quantise_v(0)

        for k in range(-1, N_GROUPS + 3):
            if in_range(k - 1):
                quantise_e(k - 1)
                coefficients(k - 1)
            if in_range(k - 2):
                for pair in range(HP):
                    difference(k - 2, pair)
                apply_gate(k - 2)
            for pair in range(HP):
                if in_range(k):
                    exponent(k, 2 * pair)
                    exponent(k, 2 * pair + 1)
                if in_range(k + 1):
                    scores(k + 1, 2 * pair)
                    scores(k + 1, 2 * pair + 1)
                if in_range(k):
                    transpose_e(k, pair)
                    if pair == 0:
                        grouped, planes = group_e_views(k, 0)
                        nc.vector.tensor_copy(out=grouped, in_=planes)
                if in_range(k - 1):
                    values(k - 1, pair)
            if in_range(k - 1):
                scale_map2(k - 1, 0)
            if in_range(k - 3):
                square_sum(k - 3, 0)
                square_sum(k - 3, 1)
                normalise(k - 3)
            if in_range(k):
                grouped, planes = group_e_views(k, 1)
                nc.scalar.copy(out=grouped, in_=planes)
            if in_range(k - 1):
                scale_map2(k - 1, 1)
            if in_range(k + 5):
                nb, h = divmod(k + 5, QT)
                if h == 0 and nb + 1 < B:
                    qkv_of[nb + 1] = load_qkv(nb + 1)
                qk_ps = transpose_qk(nb, h)
                if h == 0 or (h == 2 and nb % 2 == 0):
                    nc.vector.tensor_copy(out=qkT_of[(nb, h)][:], in_=qk_ps[:])
                else:
                    nc.scalar.copy(out=qkT_of[(nb, h)][:], in_=qk_ps[:])
                if h == QT - 2:
                    group_v(nb)
                if h == QT - 1:
                    quantise_v(nb)
            if in_range(k + 1):
                for h in range(H):
                    row_max(k + 1, h)
